import numpy as np
import ml_dtypes


def mxq(x, axis, fmt="e4m3"):
    dtype, down = {"e4m3": (ml_dtypes.float8_e4m3fn, 7), "e5m2": (ml_dtypes.float8_e5m2, 14)}[fmt]
    v = np.moveaxis(np.asarray(x, np.float32).astype(ml_dtypes.bfloat16).astype(np.float64), axis, -1)
    blocks = v.reshape(v.shape[:-1] + (-1, 32))
    amax = np.abs(blocks).max(-1, keepdims=True)
    byte = np.maximum(np.where(amax > 0, np.frexp(amax)[1] - 1 + 127, 0) - down, 1)
    scale = np.exp2(byte - 127.0)
    codes = (blocks / scale).astype(np.float32).astype(dtype).astype(np.float64)
    return np.moveaxis((codes * scale).reshape(v.shape), -1, axis)


WIDE = False


def mx_kscale(k):
    if not WIDE:
        return np.ones(k)
    levels = np.array([10, -10, 5, -5, 0])
    a = np.random.permutation(np.resize(levels, k // 512 * 4)).reshape(k // 512, 4)
    idx = np.arange(k)
    return np.exp2(a[idx // 512, idx % 128 // 32])


BF16 = ml_dtypes.bfloat16


def bf(x):
    return np.asarray(x, np.float32).astype(BF16)


def f64(x):
    return np.asarray(x).astype(np.float64)


B, D, I, O = 256, 4, 8192, 64


def setup_inputs():
    s = np.tile(mx_kscale(I), D)
    return {"x": bf(np.random.standard_normal((B, D * I)) * s),
            "W": bf(np.random.standard_normal((D * O, D * I)) / np.sqrt(I) / s[None, :])}


def reference(x, W):
    W4 = f64(W).reshape(D, O, D, I)
    Wb = np.ascontiguousarray(np.einsum('dodi->doi', W4))
    xb = f64(x).reshape(B, D, I)
    xq = mxq(xb, 2, "e4m3")
    wq = mxq(Wb, 2, "e4m3")
    out = xq.transpose(1, 0, 2) @ wq.transpose(0, 2, 1)
    return out.transpose(1, 0, 2).reshape(B, D * O)

@@ -1,0 +1,142 @@
+from contextlib import ExitStack
+
+import concourse.mybir as mybir
+from concourse.masks import make_identity
+
+BF16 = mybir.dt.bfloat16
+F32 = mybir.dt.float32
+U32 = mybir.dt.uint32
+U8 = mybir.dt.uint8
+FP8X4 = mybir.dt.float8_e4m3fn_x4
+
+P = 128
+BATCH = 256
+DETECTORS = 4
+FEATURES = 8192
+OUTS = 64
+
+B_TILES = BATCH // P
+PAIRS = DETECTORS // 2
+K_PASS = 4 * P
+K_BLOCK = 2 * K_PASS
+K_ROUND = 4 * K_BLOCK
+BLOCKS = K_ROUND // K_BLOCK
+HALVES = FEATURES // K_ROUND
+PASSES = FEATURES // K_PASS
+ROUNDS = DETECTORS * B_TILES * HALVES + PAIRS * HALVES
+VECTOR_BLOCK = 1
+
+FLOPS = 2 * BATCH * DETECTORS * FEATURES * OUTS
+BYTES = 2 * BATCH * DETECTORS * FEATURES + 2 * DETECTORS * OUTS * FEATURES + 4 * BATCH * DETECTORS * OUTS
+
+
+def tile_ensemblelinear_k_kernel(tc, x, W, out):
+    nc = tc.nc
+    with ExitStack() as ctx:
+        const = ctx.enter_context(tc.tile_pool(name="const", bufs=1))
+        raw_pool = ctx.enter_context(tc.tile_pool(name="raw", bufs=ROUNDS))
+        grouped_pool = ctx.enter_context(tc.tile_pool(name="grouped", bufs=2 * BLOCKS))
+        x_mx_pool = ctx.enter_context(tc.tile_pool(name="x_mx", bufs=3 * BLOCKS))
+        w_mx_pool = ctx.enter_context(tc.tile_pool(name="w_mx", bufs=PAIRS * HALVES * BLOCKS))
+        result_pool = ctx.enter_context(tc.tile_pool(name="result", bufs=2))
+        banks = ctx.enter_context(tc.psum_pool(name="banks", bufs=6))
+        acc_pool = ctx.enter_context(tc.psum_pool(name="acc", bufs=2))
+        ctx.enter_context(tc.manual_schedule())
+
+        ident = const.tile([P, P], F32, name="ident")
+        make_identity(nc, ident[:])
+
+        x_raw = {}
+        w_raw = {}
+        for pair in range(PAIRS):
+            for member in range(2):
+                d = 2 * pair + member
+                for bt in range(B_TILES):
+                    for half in range(HALVES):
+                        if member == 0 and bt == 0:
+                            w_tile = raw_pool.tile([P, K_ROUND], BF16, name="raw")
+                            for m in range(2):
+                                dm = 2 * pair + m
+                                k0 = dm * FEATURES + half * K_ROUND
+                                nc.sync.dma_start(
+                                    out=w_tile[m:P:2, :],
+                                    in_=W[dm * OUTS : (dm + 1) * OUTS, k0 : k0 + K_ROUND],
+                                )
+                            w_raw[pair, half] = w_tile
+                        x_tile = raw_pool.tile([P, K_ROUND], BF16, name="raw")
+                        k0 = d * FEATURES + half * K_ROUND
+                        nc.sync.dma_start(out=x_tile[:], in_=x[bt * P : (bt + 1) * P, k0 : k0 + K_ROUND])
+                        x_raw[d, bt, half] = x_tile
+
+        def transpose_and_quantise(raw, pool):
+            raw_words = raw[:].bitcast(F32)
+            grouped_tiles = []
+            for blk in range(BLOCKS):
+                bank = banks.tile([P, 4, P], F32, name="bank")
+                for i in range(4):
+                    w0 = (4 * blk + i) * P
+                    nc.tensor.transpose(bank[:, i, :], raw_words[:, w0 : w0 + P], ident[:])
+                grouped = grouped_pool.tile([P, 4 * 2 * P], BF16, name="grouped", align_bytes=64)
+                copy = nc.vector.tensor_copy if blk == VECTOR_BLOCK else nc.scalar.copy
+                copy(
+                    out=grouped[:].bitcast(F32).rearrange("p (c r u) -> p c r u", c=2, u=2),
+                    in_=bank[:].rearrange("p (c u) r -> p c r u", u=2),
+                )
+                grouped_tiles.append(grouped)
+            mx_tiles = []
+            for blk in range(BLOCKS):
+                codes = pool.tile([P, 2, P], U32, name="codes", align_bytes=64)
+                scales = pool.tile([P, 2, P], U8, name="scales", align_bytes=64)
+                nc.vector.quantize_mx(
+                    out=codes[:].rearrange("p c r -> p (c r)").bitcast(FP8X4),
+                    scales=scales[:].rearrange("p c r -> p (c r)"),
+                    in_=grouped_tiles[blk][:],
+                )
+                mx_tiles.append((codes, scales))
+            return mx_tiles
+
+        w_mx = {}
+        acc = {}
+
+        def multiply(d, bt, half, x_mx):
+            pair, member = divmod(d, 2)
+            if bt == 0 and half == 0:
+                acc[d] = acc_pool.tile([P, B_TILES, P], F32, name="acc")
+            for blk in range(BLOCKS):
+                x_codes, x_scales = x_mx[blk]
+                w_codes, w_scales = w_mx[pair, half][blk]
+                for c in range(2):
+                    k_pass = (half * BLOCKS + blk) * 2 + c
+                    nc.tensor.matmul_mx(
+                        out=acc[d][:, bt, :],
+                        lhsT=x_codes[:, c, :].bitcast(FP8X4),
+                        lhsT_scale=x_scales[:, c, :],
+                        rhs=w_codes[:, c, :].bitcast(FP8X4),
+                        rhs_scale=w_scales[:, c, :],
+                        start=(k_pass == 0),
+                        stop=(k_pass == PASSES - 1),
+                    )
+            if bt == B_TILES - 1 and half == HALVES - 1:
+                result = result_pool.tile([P, B_TILES, OUTS], F32, name="result")
+                nc.vector.tensor_copy(
+                    out=result[:],
+                    in_=acc[d][:].rearrange("p t (o m) -> p t o m", m=2)[:, :, :, member],
+                )
+                nc.sync.dma_start(
+                    out=out[:, d * OUTS : (d + 1) * OUTS].rearrange("(t p) o -> p t o", p=P),
+                    in_=result[:],
+                )
+
+        waiting = None
+        for pair in range(PAIRS):
+            for member in range(2):
+                d = 2 * pair + member
+                for bt in range(B_TILES):
+                    for half in range(HALVES):
+                        if member == 0 and bt == 0:
+                            w_mx[pair, half] = transpose_and_quantise(w_raw[pair, half], w_mx_pool)
+                        x_mx = transpose_and_quantise(x_raw[d, bt, half], x_mx_pool)
+                        if waiting is not None:
+                            multiply(*waiting)
+                        waiting = (d, bt, half, x_mx)
+        multiply(*waiting)

@@ -38,7 +38,7 @@ def tile_ensemblelinear_k_kernel(tc, x, W, out):
         grouped_pool = ctx.enter_context(tc.tile_pool(name="grouped", bufs=2 * BLOCKS))
         x_mx_pool = ctx.enter_context(tc.tile_pool(name="x_mx", bufs=3 * BLOCKS))
         w_mx_pool = ctx.enter_context(tc.tile_pool(name="w_mx", bufs=PAIRS * HALVES * BLOCKS))
-        result_pool = ctx.enter_context(tc.tile_pool(name="result", bufs=2))
+        result_pool = ctx.enter_context(tc.tile_pool(name="result", bufs=DETECTORS))
         banks = ctx.enter_context(tc.psum_pool(name="banks", bufs=6))
         acc_pool = ctx.enter_context(tc.psum_pool(name="acc", bufs=2))
         ctx.enter_context(tc.manual_schedule())

@@ -25,6 +25,8 @@ HALVES = FEATURES // K_ROUND
 PASSES = FEATURES // K_PASS
 ROUNDS = DETECTORS * B_TILES * HALVES + PAIRS * HALVES
 VECTOR_BLOCK = 1
+LAST_STEP = 2
+LAST_PIECES = 2
 
 FLOPS = 2 * BATCH * DETECTORS * FEATURES * OUTS
 BYTES = 2 * BATCH * DETECTORS * FEATURES + 2 * DETECTORS * OUTS * FEATURES + 4 * BATCH * DETECTORS * OUTS
@@ -34,11 +36,12 @@ def tile_ensemblelinear_k_kernel(tc, x, W, out):
     nc = tc.nc
     with ExitStack() as ctx:
         const = ctx.enter_context(tc.tile_pool(name="const", bufs=1))
-        raw_pool = ctx.enter_context(tc.tile_pool(name="raw", bufs=ROUNDS))
+        raw_pool = ctx.enter_context(tc.tile_pool(name="raw", bufs=ROUNDS - 1))
+        last_pool = ctx.enter_context(tc.tile_pool(name="last", bufs=LAST_PIECES))
         grouped_pool = ctx.enter_context(tc.tile_pool(name="grouped", bufs=2 * BLOCKS))
-        x_mx_pool = ctx.enter_context(tc.tile_pool(name="x_mx", bufs=3 * BLOCKS))
+        x_mx_pool = ctx.enter_context(tc.tile_pool(name="x_mx", bufs=4 * BLOCKS))
         w_mx_pool = ctx.enter_context(tc.tile_pool(name="w_mx", bufs=PAIRS * HALVES * BLOCKS))
-        result_pool = ctx.enter_context(tc.tile_pool(name="result", bufs=DETECTORS))
+        result_pool = ctx.enter_context(tc.tile_pool(name="result", bufs=DETECTORS * B_TILES))
         banks = ctx.enter_context(tc.psum_pool(name="banks", bufs=6))
         acc_pool = ctx.enter_context(tc.psum_pool(name="acc", bufs=2))
         ctx.enter_context(tc.manual_schedule())
@@ -62,20 +65,29 @@ def tile_ensemblelinear_k_kernel(tc, x, W, out):
                                     out=w_tile[m:P:2, :],
                                     in_=W[dm * OUTS : (dm + 1) * OUTS, k0 : k0 + K_ROUND],
                                 )
-                            w_raw[pair, half] = w_tile
-                        x_tile = raw_pool.tile([P, K_ROUND], BF16, name="raw")
+                            w_raw[pair, half] = [w_tile[:, blk * K_BLOCK : (blk + 1) * K_BLOCK] for blk in range(BLOCKS)]
                         k0 = d * FEATURES + half * K_ROUND
-                        nc.sync.dma_start(out=x_tile[:], in_=x[bt * P : (bt + 1) * P, k0 : k0 + K_ROUND])
-                        x_raw[d, bt, half] = x_tile
+                        if (d, bt, half) == (DETECTORS - 1, B_TILES - 1, HALVES - 1):
+                            x_raw[d, bt, half] = []
+                            k_piece = K_ROUND // LAST_PIECES
+                            for piece in range(LAST_PIECES):
+                                x_piece = last_pool.tile([P, k_piece], BF16, name="last")
+                                kp = k0 + piece * k_piece
+                                nc.sync.dma_start(out=x_piece[:], in_=x[bt * P : (bt + 1) * P, kp : kp + k_piece])
+                                for blk in range(k_piece // K_BLOCK):
+                                    x_raw[d, bt, half].append(x_piece[:, blk * K_BLOCK : (blk + 1) * K_BLOCK])
+                        else:
+                            x_tile = raw_pool.tile([P, K_ROUND], BF16, name="raw")
+                            nc.sync.dma_start(out=x_tile[:], in_=x[bt * P : (bt + 1) * P, k0 : k0 + K_ROUND])
+                            x_raw[d, bt, half] = [x_tile[:, blk * K_BLOCK : (blk + 1) * K_BLOCK] for blk in range(BLOCKS)]
 
         def transpose_and_quantise(raw, pool):
-            raw_words = raw[:].bitcast(F32)
             grouped_tiles = []
             for blk in range(BLOCKS):
                 bank = banks.tile([P, 4, P], F32, name="bank")
+                raw_words = raw[blk].bitcast(F32)
                 for i in range(4):
-                    w0 = (4 * blk + i) * P
-                    nc.tensor.transpose(bank[:, i, :], raw_words[:, w0 : w0 + P], ident[:])
+                    nc.tensor.transpose(bank[:, i, :], raw_words[:, i * P : (i + 1) * P], ident[:])
                 grouped = grouped_pool.tile([P, 4 * 2 * P], BF16, name="grouped", align_bytes=64)
                 copy = nc.vector.tensor_copy if blk == VECTOR_BLOCK else nc.scalar.copy
                 copy(
@@ -100,15 +112,15 @@ def tile_ensemblelinear_k_kernel(tc, x, W, out):
 
         def multiply(d, bt, half, x_mx):
             pair, member = divmod(d, 2)
-            if bt == 0 and half == 0:
-                acc[d] = acc_pool.tile([P, B_TILES, P], F32, name="acc")
+            if half == 0:
+                acc[d, bt] = acc_pool.tile([P, P], F32, name="acc")
             for blk in range(BLOCKS):
                 x_codes, x_scales = x_mx[blk]
                 w_codes, w_scales = w_mx[pair, half][blk]
                 for c in range(2):
                     k_pass = (half * BLOCKS + blk) * 2 + c
                     nc.tensor.matmul_mx(
-                        out=acc[d][:, bt, :],
+                        out=acc[d, bt][:],
                         lhsT=x_codes[:, c, :].bitcast(FP8X4),
                         lhsT_scale=x_scales[:, c, :],
                         rhs=w_codes[:, c, :].bitcast(FP8X4),
@@ -116,27 +128,34 @@ def tile_ensemblelinear_k_kernel(tc, x, W, out):
                         start=(k_pass == 0),
                         stop=(k_pass == PASSES - 1),
                     )
-            if bt == B_TILES - 1 and half == HALVES - 1:
-                result = result_pool.tile([P, B_TILES, OUTS], F32, name="result")
+            if half == HALVES - 1:
+                result = result_pool.tile([P, OUTS], F32, name="result")
                 nc.vector.tensor_copy(
                     out=result[:],
-                    in_=acc[d][:].rearrange("p t (o m) -> p t o m", m=2)[:, :, :, member],
+                    in_=acc[d, bt][:].rearrange("p (o m) -> p o m", m=2)[:, :, member],
                 )
-                nc.sync.dma_start(
-                    out=out[:, d * OUTS : (d + 1) * OUTS].rearrange("(t p) o -> p t o", p=P),
-                    in_=result[:],
-                )
+                nc.sync.dma_start(out=out[bt * P : (bt + 1) * P, d * OUTS : (d + 1) * OUTS], in_=result[:])
 
-        waiting = None
+        rounds = []
         for pair in range(PAIRS):
             for member in range(2):
                 d = 2 * pair + member
                 for bt in range(B_TILES):
                     for half in range(HALVES):
                         if member == 0 and bt == 0:
-                            w_mx[pair, half] = transpose_and_quantise(w_raw[pair, half], w_mx_pool)
-                        x_mx = transpose_and_quantise(x_raw[d, bt, half], x_mx_pool)
-                        if waiting is not None:
-                            multiply(*waiting)
-                        waiting = (d, bt, half, x_mx)
-        multiply(*waiting)
+                            rounds.append(("w", pair, half))
+                        rounds.append(("x", d, bt, half))
+        steps = [[r] for r in rounds[: len(rounds) - LAST_STEP]] + [rounds[len(rounds) - LAST_STEP :]]
+        waiting = []
+        for step in steps:
+            quantised = []
+            for r in step:
+                if r[0] == "w":
+                    w_mx[r[1], r[2]] = transpose_and_quantise(w_raw[r[1], r[2]], w_mx_pool)
+                else:
+                    quantised.append((r[1], r[2], r[3], transpose_and_quantise(x_raw[r[1], r[2], r[3]], x_mx_pool)))
+            for ready in waiting:
+                multiply(*ready)
+            waiting = quantised
+        for ready in waiting:
+            multiply(*ready)

@@ -26,7 +26,7 @@ PASSES = FEATURES // K_PASS
 ROUNDS = DETECTORS * B_TILES * HALVES + PAIRS * HALVES
 VECTOR_BLOCK = 1
 LAST_STEP = 2
-LAST_PIECES = 2
+LAST_PIECES = 4
 
 FLOPS = 2 * BATCH * DETECTORS * FEATURES * OUTS
 BYTES = 2 * BATCH * DETECTORS * FEATURES + 2 * DETECTORS * OUTS * FEATURES + 4 * BATCH * DETECTORS * OUTS

from contextlib import ExitStack

import concourse.mybir as mybir
from concourse.masks import make_identity

BF16 = mybir.dt.bfloat16
F32 = mybir.dt.float32
U32 = mybir.dt.uint32
U8 = mybir.dt.uint8
FP8X4 = mybir.dt.float8_e4m3fn_x4

P = 128
BATCH = 256
DETECTORS = 4
FEATURES = 8192
OUTS = 64

B_TILES = BATCH // P
PAIRS = DETECTORS // 2
K_PASS = 4 * P
K_BLOCK = 2 * K_PASS
K_ROUND = 4 * K_BLOCK
BLOCKS = K_ROUND // K_BLOCK
HALVES = FEATURES // K_ROUND
PASSES = FEATURES // K_PASS
ROUNDS = DETECTORS * B_TILES * HALVES + PAIRS * HALVES
VECTOR_BLOCK = 1
LAST_STEP = 2
LAST_PIECES = 4

FLOPS = 2 * BATCH * DETECTORS * FEATURES * OUTS
BYTES = 2 * BATCH * DETECTORS * FEATURES + 2 * DETECTORS * OUTS * FEATURES + 4 * BATCH * DETECTORS * OUTS


def tile_ensemblelinear_k_kernel(tc, x, W, out):
    nc = tc.nc
    with ExitStack() as ctx:
        const = ctx.enter_context(tc.tile_pool(name="const", bufs=1))
        raw_pool = ctx.enter_context(tc.tile_pool(name="raw", bufs=ROUNDS - 1))
        last_pool = ctx.enter_context(tc.tile_pool(name="last", bufs=LAST_PIECES))
        grouped_pool = ctx.enter_context(tc.tile_pool(name="grouped", bufs=2 * BLOCKS))
        x_mx_pool = ctx.enter_context(tc.tile_pool(name="x_mx", bufs=4 * BLOCKS))
        w_mx_pool = ctx.enter_context(tc.tile_pool(name="w_mx", bufs=PAIRS * HALVES * BLOCKS))
        result_pool = ctx.enter_context(tc.tile_pool(name="result", bufs=DETECTORS * B_TILES))
        banks = ctx.enter_context(tc.psum_pool(name="banks", bufs=6))
        acc_pool = ctx.enter_context(tc.psum_pool(name="acc", bufs=2))
        ctx.enter_context(tc.manual_schedule())

        ident = const.tile([P, P], F32, name="ident")
        make_identity(nc, ident[:])

        x_raw = {}
        w_raw = {}
        for pair in range(PAIRS):
            for member in range(2):
                d = 2 * pair + member
                for bt in range(B_TILES):
                    for half in range(HALVES):
                        if member == 0 and bt == 0:
                            w_tile = raw_pool.tile([P, K_ROUND], BF16, name="raw")
                            for m in range(2):
                                dm = 2 * pair + m
                                k0 = dm * FEATURES + half * K_ROUND
                                nc.sync.dma_start(
                                    out=w_tile[m:P:2, :],
                                    in_=W[dm * OUTS : (dm + 1) * OUTS, k0 : k0 + K_ROUND],
                                )
                            w_raw[pair, half] = [w_tile[:, blk * K_BLOCK : (blk + 1) * K_BLOCK] for blk in range(BLOCKS)]
                        k0 = d * FEATURES + half * K_ROUND
                        if (d, bt, half) == (DETECTORS - 1, B_TILES - 1, HALVES - 1):
                            x_raw[d, bt, half] = []
                            k_piece = K_ROUND // LAST_PIECES
                            for piece in range(LAST_PIECES):
                                x_piece = last_pool.tile([P, k_piece], BF16, name="last")
                                kp = k0 + piece * k_piece
                                nc.sync.dma_start(out=x_piece[:], in_=x[bt * P : (bt + 1) * P, kp : kp + k_piece])
                                for blk in range(k_piece // K_BLOCK):
                                    x_raw[d, bt, half].append(x_piece[:, blk * K_BLOCK : (blk + 1) * K_BLOCK])
                        else:
                            x_tile = raw_pool.tile([P, K_ROUND], BF16, name="raw")
                            nc.sync.dma_start(out=x_tile[:], in_=x[bt * P : (bt + 1) * P, k0 : k0 + K_ROUND])
                            x_raw[d, bt, half] = [x_tile[:, blk * K_BLOCK : (blk + 1) * K_BLOCK] for blk in range(BLOCKS)]

        def transpose_and_quantise(raw, pool):
            grouped_tiles = []
            for blk in range(BLOCKS):
                bank = banks.tile([P, 4, P], F32, name="bank")
                raw_words = raw[blk].bitcast(F32)
                for i in range(4):
                    nc.tensor.transpose(bank[:, i, :], raw_words[:, i * P : (i + 1) * P], ident[:])
                grouped = grouped_pool.tile([P, 4 * 2 * P], BF16, name="grouped", align_bytes=64)
                copy = nc.vector.tensor_copy if blk == VECTOR_BLOCK else nc.scalar.copy
                copy(
                    out=grouped[:].bitcast(F32).rearrange("p (c r u) -> p c r u", c=2, u=2),
                    in_=bank[:].rearrange("p (c u) r -> p c r u", u=2),
                )
                grouped_tiles.append(grouped)
            mx_tiles = []
            for blk in range(BLOCKS):
                codes = pool.tile([P, 2, P], U32, name="codes", align_bytes=64)
                scales = pool.tile([P, 2, P], U8, name="scales", align_bytes=64)
                nc.vector.quantize_mx(
                    out=codes[:].rearrange("p c r -> p (c r)").bitcast(FP8X4),
                    scales=scales[:].rearrange("p c r -> p (c r)"),
                    in_=grouped_tiles[blk][:],
                )
                mx_tiles.append((codes, scales))
            return mx_tiles

        w_mx = {}
        acc = {}

        def multiply(d, bt, half, x_mx):
            pair, member = divmod(d, 2)
            if half == 0:
                acc[d, bt] = acc_pool.tile([P, P], F32, name="acc")
            for blk in range(BLOCKS):
                x_codes, x_scales = x_mx[blk]
                w_codes, w_scales = w_mx[pair, half][blk]
                for c in range(2):
                    k_pass = (half * BLOCKS + blk) * 2 + c
                    nc.tensor.matmul_mx(
                        out=acc[d, bt][:],
                        lhsT=x_codes[:, c, :].bitcast(FP8X4),
                        lhsT_scale=x_scales[:, c, :],
                        rhs=w_codes[:, c, :].bitcast(FP8X4),
                        rhs_scale=w_scales[:, c, :],
                        start=(k_pass == 0),
                        stop=(k_pass == PASSES - 1),
                    )
            if half == HALVES - 1:
                result = result_pool.tile([P, OUTS], F32, name="result")
                nc.vector.tensor_copy(
                    out=result[:],
                    in_=acc[d, bt][:].rearrange("p (o m) -> p o m", m=2)[:, :, member],
                )
                nc.sync.dma_start(out=out[bt * P : (bt + 1) * P, d * OUTS : (d + 1) * OUTS], in_=result[:])

        rounds = []
        for pair in range(PAIRS):
            for member in range(2):
                d = 2 * pair + member
                for bt in range(B_TILES):
                    for half in range(HALVES):
                        if member == 0 and bt == 0:
                            rounds.append(("w", pair, half))
                        rounds.append(("x", d, bt, half))
        steps = [[r] for r in rounds[: len(rounds) - LAST_STEP]] + [rounds[len(rounds) - LAST_STEP :]]
        waiting = []
        for step in steps:
            quantised = []
            for r in step:
                if r[0] == "w":
                    w_mx[r[1], r[2]] = transpose_and_quantise(w_raw[r[1], r[2]], w_mx_pool)
                else:
                    quantised.append((r[1], r[2], r[3], transpose_and_quantise(x_raw[r[1], r[2], r[3]], x_mx_pool)))
            for ready in waiting:
                multiply(*ready)
            waiting = quantised
        for ready in waiting:
            multiply(*ready)
